import numpy as np
import ml_dtypes


def mxq(x, axis, fmt="e4m3"):
    dtype, down = {"e4m3": (ml_dtypes.float8_e4m3fn, 7), "e5m2": (ml_dtypes.float8_e5m2, 14)}[fmt]
    v = np.moveaxis(np.asarray(x, np.float32).astype(ml_dtypes.bfloat16).astype(np.float64), axis, -1)
    blocks = v.reshape(v.shape[:-1] + (-1, 32))
    amax = np.abs(blocks).max(-1, keepdims=True)
    byte = np.maximum(np.where(amax > 0, np.frexp(amax)[1] - 1 + 127, 0) - down, 1)
    scale = np.exp2(byte - 127.0)
    codes = (blocks / scale).astype(np.float32).astype(dtype).astype(np.float64)
    return np.moveaxis((codes * scale).reshape(v.shape), -1, axis)


WIDE = False


def mx_kscale(k):
    if not WIDE:
        return np.ones(k)
    levels = np.array([10, -10, 5, -5, 0])
    if k % 512:
        return np.exp2(np.random.permutation(np.resize(levels, k // 32))).repeat(32)
    a = np.empty((k // 512, 16))
    for p in range(k // 512):
        a[p, :8] = np.random.permutation(np.resize(levels, 8))
        for g in range(8):
            far = levels[np.abs(levels - a[p, g]) >= 10]
            a[p, g + 8] = far[np.random.randint(len(far))]
    return np.exp2(a.ravel()).repeat(32)


BF16 = ml_dtypes.bfloat16


def bf(x):
    return np.asarray(x, np.float32).astype(BF16)


def f64(x):
    return np.asarray(x).astype(np.float64)


B, H, W, C, NH, WS, SHIFT, MR = 4, 64, 64, 256, 4, 32, 16, 4
HD = C // NH
WS2 = WS * WS
NWH, NWW = H // WS, W // WS
EPS = 1e-5
G2 = 0.1


def layer_norm(v, w, b):
    mu = v.mean(-1, keepdims=True)
    var = ((v - mu) ** 2).mean(-1, keepdims=True)
    return (v - mu) * (1.0 / np.sqrt(var + EPS)) * w + b


def setup_inputs():
    s = mx_kscale(WS2)
    u = (s / s.max()) ** 2
    um = np.tile(u.reshape(WS, WS), (NWH, NWW)).reshape(1, H * W, 1)
    d = u * np.sqrt((G2 + EPS) / (G2 * u * u + EPS))
    g = np.exp2(-7.5 * np.random.random_sample((B, H * W, 1)))
    x = (np.random.standard_normal((B, H * W, C)) + 0.5 * np.random.standard_normal((B, H * W, 1))) * g * um
    return {"x": bf(x),
            "norm1_w": bf(1.0 + 0.2 * np.random.standard_normal(C)),
            "norm1_b": bf(0.2 * np.random.standard_normal(C) * d.min()),
            "spatial_w": bf(np.random.standard_normal((NH, WS2, WS2)) / np.sqrt(WS2) / d[None, None, :]),
            "spatial_b": bf(0.3 * np.random.standard_normal((NH, WS2)))}


def reference(x, norm1_w, norm1_b, spatial_w, spatial_b):
    x = f64(x)
    xn = layer_norm(x, f64(norm1_w), f64(norm1_b))
    win = xn.reshape(B, NWH, WS, NWW, WS, C).transpose(0, 1, 3, 2, 4, 5).reshape(-1, WS2, NH, HD)
    wh = win.transpose(0, 2, 1, 3)
    out = (mxq(f64(spatial_w), 2, "e4m3")[None] @ mxq(wh, 2, "e4m3")) + f64(spatial_b)[None, :, :, None]
    w2 = out.transpose(0, 2, 1, 3).reshape(B, NWH, NWW, WS, WS, C)
    xs2 = w2.transpose(0, 1, 3, 2, 4, 5).reshape(B, H * W, C)
    return x + xs2

@@ -1,0 +1,320 @@
+from contextlib import ExitStack
+
+import concourse.mybir as mybir
+from concourse.masks import make_identity
+
+F32 = mybir.dt.float32
+BF16 = mybir.dt.bfloat16
+U32 = mybir.dt.uint32
+U8 = mybir.dt.uint8
+FP8X4 = mybir.dt.float8_e4m3fn_x4
+ALU = mybir.AluOpType
+ACT = mybir.ActivationFunctionType
+
+P = 128
+PACK = 4
+IMAGES = 4
+WINDOWS = 4
+TOKENS = 1024
+PASSES = TOKENS // (P * PACK)
+CHANNELS = 256
+HALVES = CHANNELS // P
+HEADS = 4
+HEAD_DIM = CHANNELS // HEADS
+EPS = 1e-5
+COLS = WINDOWS * HEAD_DIM
+BATCH = WINDOWS * PACK
+TILES_PER_IMAGE = PASSES * WINDOWS
+TILES = IMAGES * TILES_PER_IMAGE
+UNITS = TILES
+KINDS = PASSES * PACK
+PAIRS = HEADS // 2
+CHUNKS = KINDS * PAIRS
+PSUM_BANKS = 8
+
+STATS_LEAD = 8
+TURN_LAG = 1
+BACK_LAG = 3
+QUANT_LAG = BACK_LAG + 1
+MIX_LAG = TILES_PER_IMAGE - 1 + QUANT_LAG + 1
+OUT_LAG = MIX_LAG + 1
+LOAD_LEAD = 4
+TILES_PER_LOAD = 2
+
+FLOPS = 2 * IMAGES * WINDOWS * HEADS * TOKENS * TOKENS * HEAD_DIM
+
+
+def tile_swinmlpblocknew_pa_t_kernel(tc, x, norm1_w, norm1_b, spatial_w, spatial_b, out):
+    nc = tc.nc
+
+    cut = "b (wr g r wc q j) c -> b wr wc g r q (j c)"
+    sizes = dict(wr=2, g=PASSES, r=16, wc=2, q=8, j=PACK)
+    x_cut = x.rearrange(cut, **sizes)
+    out_cut = out.rearrange(cut, **sizes)
+
+    with ExitStack() as ctx:
+        const = ctx.enter_context(tc.tile_pool(name="const", bufs=1))
+        images = ctx.enter_context(tc.tile_pool(name="images", bufs=1))
+        w_keep = ctx.enter_context(tc.tile_pool(name="w_keep", bufs=1))
+        w_stage = ctx.enter_context(tc.tile_pool(name="w_stage", bufs=2))
+        stats = ctx.enter_context(tc.tile_pool(name="stats", bufs=4))
+        norm = ctx.enter_context(tc.tile_pool(name="norm", bufs=3))
+        x_stage = ctx.enter_context(tc.tile_pool(name="x_stage", bufs=2))
+        x_keep = ctx.enter_context(tc.tile_pool(name="x_keep", bufs=2 * PASSES))
+        results = ctx.enter_context(tc.tile_pool(name="results", bufs=2))
+        banks = ctx.enter_context(tc.psum_pool(name="banks", bufs=PSUM_BANKS))
+        ctx.enter_context(tc.manual_schedule())
+
+        def place(i):
+            batch, n = i // WINDOWS, i % WINDOWS
+            return batch, batch // PASSES, batch % PASSES, n
+
+        x_sb = [images.tile([P, TILES_PER_IMAGE * PACK * CHANNELS], BF16, name="x_sb%d" % b) for b in range(IMAGES)]
+
+        def x_tokens(b):
+            return x_sb[b][:].rearrange("p (n g j c) -> p n g j c", n=WINDOWS, g=PASSES, j=PACK)
+
+        def load_tile(i):
+            batch, b, g, n = place(i)
+            rows = x_sb[b][:].rearrange("p (n g f) -> p n g f", n=WINDOWS, g=PASSES)
+            nc.sync.dma_start(out=rows[:, n, g, :], in_=x_cut[b, n // 2, n % 2, g])
+
+        for i in range(TILES_PER_IMAGE):
+            load_tile(i)
+
+        ident_f32 = const.tile([P, P], F32, name="ident_f32")
+        make_identity(nc, ident_f32[:])
+        ident_bf16 = const.tile([P, P], BF16, name="ident_bf16")
+        make_identity(nc, ident_bf16[:])
+
+        bias_rows = const.tile([P, P * PACK], BF16, name="bias_rows")
+        nc.scalar.dma_start(
+            out=bias_rows[0 : HEADS * PASSES, :], in_=spatial_b.rearrange("h (g f) -> (h g) f", g=PASSES)
+        )
+        rows = const.tile([P, PACK + 1, P], BF16, name="rows")
+        nc.gpsimd.memset(rows[:], 0.0)
+        nc.scalar.dma_start(out=rows[0:HALVES, PACK, :], in_=norm1_w.rearrange("(a c) -> a c", a=HALVES))
+        nc.scalar.dma_start(out=rows[HALVES : 2 * HALVES, PACK, :], in_=norm1_b.rearrange("(a c) -> a c", a=HALVES))
+        nc.gpsimd.tensor_copy(
+            out=rows[0 : HEADS * PASSES, 0:PACK, :],
+            in_=bias_rows[0 : HEADS * PASSES, :].rearrange("r (p j) -> r j p", j=PACK),
+        )
+        rows_turned = banks.tile([P, 8, P], BF16, tag="bank", name="rows_turned")
+        for plane in range(PACK + 1):
+            nc.tensor.transpose(rows_turned[:, plane, :], rows[:, plane, :], ident_bf16[:])
+        columns = const.tile([P, PACK + 1, HEADS * PASSES], F32, name="columns")
+        nc.scalar.copy(out=columns[:], in_=rows_turned[:, 0 : PACK + 1, 0 : HEADS * PASSES])
+
+        def bias_column(h, g, j):
+            return columns[:, j, PASSES * h + g : PASSES * h + g + 1]
+
+        def gain_column(half):
+            return columns[:, PACK, half : half + 1]
+
+        def shift_column(half):
+            return columns[:, PACK, HALVES + half : HALVES + half + 1]
+
+        w_codes = w_keep.tile([P, CHUNKS, 2 * PASSES * P], U32, name="w_codes", align_bytes=64)
+        w_scales = w_keep.tile([P, CHUNKS, 2 * PASSES * P], U8, name="w_scales", align_bytes=64)
+        w_raw = {}
+        w_grouped = {}
+
+        def load_weights(chunk):
+            kind, pair = chunk // PAIRS, chunk % PAIRS
+            g_out, j = kind // PACK, kind % PACK
+            w_raw[chunk] = w_stage.tile([P, 2, TOKENS], BF16, name="w_raw", bufs=LOAD_LEAD)
+            rows_of_pass = spatial_w[2 * pair : 2 * pair + 2, g_out * P * PACK : (g_out + 1) * P * PACK, :]
+            nc.sync.dma_start(out=w_raw[chunk][:], in_=rows_of_pass.rearrange("h (p j) t -> j p h t", j=PACK)[j])
+
+        def turn_weights(chunk):
+            w_grouped[chunk] = w_stage.tile([P, 2 * PASSES * P * PACK], BF16, name="w_grouped", align_bytes=64)
+            words = w_raw[chunk][:].bitcast(F32).rearrange("p h (g q u) -> p h g q u", g=PASSES, u=2)
+            grouped_words = w_grouped[chunk][:].bitcast(F32).rearrange("q (h g p u) -> q h g p u", h=2, g=PASSES, u=2)
+            for side in range(2):
+                bank = banks.tile([P, PASSES, 2, P], F32, tag="bank", name="w_bank")
+                for g in range(PASSES):
+                    for u in range(2):
+                        nc.tensor.transpose(bank[:, g, u, :], words[:, side, g, :, u], ident_f32[:])
+                nc.scalar.copy(out=grouped_words[:, side], in_=bank[:].rearrange("q g u p -> q g p u"))
+
+        def quantise_weights(chunk):
+            nc.vector.quantize_mx(
+                out=w_codes[:, chunk, :].bitcast(FP8X4), scales=w_scales[:, chunk, :], in_=w_grouped[chunk][:]
+            )
+
+        halves = {}
+        minus_mean = {}
+        variance = {}
+        std = {}
+        rstd = {}
+
+        def tile_statistics(i):
+            batch, b, g, n = place(i)
+            if n == 0:
+                halves[batch] = stats.tile([P, BATCH, 6], F32, name="halves")
+            for j in range(PACK):
+                nc.vector.bn_stats(out=halves[batch][:, PACK * n + j, :], in_=x_tokens(b)[:, n, g, j, :])
+
+        def deviation(batch):
+            even_odd = halves[batch]
+            both = stats.tile([P, BATCH, 2], F32, name="both")
+            nc.vector.tensor_tensor(out=both[:], in0=even_odd[:, :, 1:3], in1=even_odd[:, :, 4:6], op=ALU.add)
+            gap = stats.tile([P, BATCH, 1], F32, name="gap")
+            nc.vector.tensor_tensor(out=gap[:], in0=even_odd[:, :, 1:2], in1=even_odd[:, :, 4:5], op=ALU.subtract)
+            minus_mean[batch] = stats.tile([P, BATCH, 1], F32, name="minus_mean")
+            nc.vector.tensor_scalar(
+                out=minus_mean[batch][:], in0=both[:, :, 0:1], scalar1=-0.5, scalar2=None, op0=ALU.mult
+            )
+            gap_sq = stats.tile([P, BATCH, 1], F32, name="gap_sq")
+            nc.vector.tensor_tensor(out=gap_sq[:], in0=gap[:], in1=gap[:], op=ALU.mult)
+            within = stats.tile([P, BATCH, 1], F32, name="within")
+            nc.vector.tensor_scalar(
+                out=within[:], in0=both[:, :, 1:2], scalar1=1.0 / CHANNELS, scalar2=EPS, op0=ALU.mult, op1=ALU.add
+            )
+            var_eps = stats.tile([P, BATCH, 1], F32, name="var_eps")
+            nc.vector.scalar_tensor_tensor(
+                out=var_eps[:], in0=gap_sq[:], scalar=0.25, in1=within[:], op0=ALU.mult, op1=ALU.add
+            )
+            variance[batch] = var_eps
+
+        def root(batch):
+            std[batch] = stats.tile([P, BATCH, 1], F32, name="std")
+            nc.scalar.activation(out=std[batch][:], in_=variance[batch][:], func=ACT.Sqrt)
+
+        def inverse_deviation(batch):
+            rstd[batch] = stats.tile([P, BATCH, 1], F32, name="rstd")
+            nc.vector.reciprocal(out=rstd[batch][:], in_=std[batch][:])
+
+        x_hat = {}
+        xn_turned = {}
+        x_grouped = {}
+        x_codes = {}
+
+        def normalise(i):
+            batch, b, g, n = place(i)
+            x_hat[i] = norm.tile([P, PACK, CHANNELS], F32, name="x_hat")
+            for j in range(PACK):
+                nc.gpsimd.tensor_scalar(
+                    out=x_hat[i][:, j, :],
+                    in0=x_tokens(b)[:, n, g, j, :],
+                    scalar1=minus_mean[batch][:, PACK * n + j, :],
+                    scalar2=rstd[batch][:, PACK * n + j, :],
+                    op0=ALU.add,
+                    op1=ALU.mult,
+                )
+
+        def to_channels(i):
+            xn_turned[i] = norm.tile([P, HALVES, 2, P, 2], BF16, name="xn_turned")
+            for half in range(HALVES):
+                bank = banks.tile([P, PACK, P], F32, tag="bank", name="hat_bank")
+                for j in range(PACK):
+                    nc.tensor.transpose(bank[:, j, :], x_hat[i][:, j, half * P : (half + 1) * P], ident_f32[:])
+                nc.scalar.activation(
+                    out=xn_turned[i][:, half],
+                    in_=bank[:].rearrange("c (u e) p -> c u p e", u=2),
+                    func=ACT.Identity,
+                    bias=shift_column(half),
+                    scale=gain_column(half),
+                )
+
+        def to_tokens(i):
+            batch, b, g, n = place(i)
+            words = xn_turned[i][:].rearrange("c a u p e -> c (a u p e)").bitcast(F32)
+            words = words.rearrange("c (a u q) -> c a u q", a=HALVES, u=2)
+            bank = banks.tile([P, 2, CHANNELS], F32, tag="bank", name="xn_bank")
+            for u in range(2):
+                for half in range(HALVES):
+                    nc.tensor.transpose(bank[:, u, half * P : (half + 1) * P], words[:, half, u, :], ident_f32[:])
+            if n == 0:
+                x_grouped[batch] = x_stage.tile([P, HEADS * COLS * PACK], BF16, name="x_grouped", align_bytes=64)
+            grouped_words = (
+                x_grouped[batch][:].bitcast(F32).rearrange("q (h n d u) -> q h n d u", h=HEADS, n=WINDOWS, u=2)
+            )
+            nc.scalar.copy(out=grouped_words[:, :, n], in_=bank[:].rearrange("q u (h d) -> q h d u", h=HEADS))
+
+        def quantise_tokens(batch):
+            codes = x_keep.tile([P, HEADS * COLS], U32, name="x_codes", align_bytes=64)
+            scales = x_keep.tile([P, HEADS * COLS], U8, name="x_scales", align_bytes=64)
+            nc.vector.quantize_mx(out=codes[:].bitcast(FP8X4), scales=scales[:], in_=x_grouped[batch][:])
+            x_codes[batch] = (codes, scales)
+
+        sums = {}
+        result = {}
+
+        def multiply(unit):
+            b, kind = unit // KINDS, unit % KINDS
+            for pair in range(PAIRS):
+                chunk = PAIRS * kind + pair
+                sums[unit, pair] = banks.tile([P, 2, COLS], F32, tag="bank", name="sum_bank")
+                for side in range(2):
+                    h = 2 * pair + side
+                    for g in range(PASSES):
+                        codes, scales = x_codes[PASSES * b + g]
+                        w_cols = slice((PASSES * side + g) * P, (PASSES * side + g + 1) * P)
+                        x_cols = slice(h * COLS, (h + 1) * COLS)
+                        nc.tensor.matmul_mx(
+                            out=sums[unit, pair][:, side, :],
+                            lhsT=w_codes[:, chunk, w_cols].bitcast(FP8X4),
+                            lhsT_scale=w_scales[:, chunk, w_cols],
+                            rhs=codes[:, x_cols].bitcast(FP8X4),
+                            rhs_scale=scales[:, x_cols],
+                            start=(g == 0),
+                            stop=(g == PASSES - 1),
+                        )
+
+        def add_and_store(unit):
+            b, kind = unit // KINDS, unit % KINDS
+            g_out, j = kind // PACK, kind % PACK
+            if j == 0:
+                result[b, g_out] = results.tile([P, WINDOWS, PACK, CHANNELS], F32, name="result")
+            res = result[b, g_out]
+            for h in range(HEADS):
+                channels = slice(h * HEAD_DIM, (h + 1) * HEAD_DIM)
+                nc.vector.scalar_tensor_tensor(
+                    out=res[:, :, j, channels],
+                    in0=sums[unit, h // 2][:, h % 2, :].rearrange("p (n d) -> p n d", n=WINDOWS),
+                    scalar=bias_column(h, g_out, j),
+                    in1=x_tokens(b)[:, :, g_out, j, channels],
+                    op0=ALU.add,
+                    op1=ALU.add,
+                )
+            if j == PACK - 1:
+                for n in range(WINDOWS):
+                    nc.sync.dma_start(
+                        out=out_cut[b, n // 2, n % 2, g_out], in_=res[:, n].rearrange("p j c -> p (j c)")
+                    )
+
+        def last_of_batch(i):
+            return 0 <= i < TILES and i % WINDOWS == WINDOWS - 1
+
+        for step in range(-STATS_LEAD, UNITS + OUT_LAG):
+            if last_of_batch(step + STATS_LEAD - 2):
+                inverse_deviation((step + STATS_LEAD - 2) // WINDOWS)
+            if 0 <= step - OUT_LAG:
+                add_and_store(step - OUT_LAG)
+            if last_of_batch(step - QUANT_LAG):
+                quantise_tokens((step - QUANT_LAG) // WINDOWS)
+            if 0 <= step - 1 < CHUNKS:
+                quantise_weights(step - 1)
+            if last_of_batch(step + STATS_LEAD - 1):
+                root((step + STATS_LEAD - 1) // WINDOWS)
+            if 0 <= step - BACK_LAG < TILES:
+                to_tokens(step - BACK_LAG)
+            if 0 <= step - TURN_LAG < TILES:
+                to_channels(step - TURN_LAG)
+            if 0 <= step < CHUNKS:
+                turn_weights(step)
+            if 0 <= step - MIX_LAG < UNITS:
+                multiply(step - MIX_LAG)
+            if 0 <= step < TILES:
+                normalise(step)
+            if step + STATS_LEAD < TILES:
+                tile_statistics(step + STATS_LEAD)
+                if last_of_batch(step + STATS_LEAD):
+                    deviation((step + STATS_LEAD) // WINDOWS)
+            chunk = step + LOAD_LEAD
+            if 0 <= chunk < CHUNKS:
+                load_weights(chunk)
+                first = TILES_PER_IMAGE + TILES_PER_LOAD * chunk
+                for i in range(first, min(first + TILES_PER_LOAD, TILES)):
+                    load_tile(i)

@@ -142,48 +142,46 @@ def tile_swinmlpblocknew_pa_t_kernel(tc, x, norm1_w, norm1_b, spatial_w, spatial
                 out=w_codes[:, chunk, :].bitcast(FP8X4), scales=w_scales[:, chunk, :], in_=w_grouped[chunk][:]
             )
 
-        halves = {}
-        minus_mean = {}
-        variance = {}
+        moments = {}
         std = {}
         rstd = {}
+        shift = {}
 
         def tile_statistics(i):
             batch, b, g, n = place(i)
             if n == 0:
-                halves[batch] = stats.tile([P, BATCH, 6], F32, name="halves")
-            for j in range(PACK):
-                nc.vector.bn_stats(out=halves[batch][:, PACK * n + j, :], in_=x_tokens(b)[:, n, g, j, :])
-
-        def deviation(batch):
-            even_odd = halves[batch]
-            both = stats.tile([P, BATCH, 2], F32, name="both")
-            nc.vector.tensor_tensor(out=both[:], in0=even_odd[:, :, 1:3], in1=even_odd[:, :, 4:6], op=ALU.add)
-            gap = stats.tile([P, BATCH, 1], F32, name="gap")
-            nc.vector.tensor_tensor(out=gap[:], in0=even_odd[:, :, 1:2], in1=even_odd[:, :, 4:5], op=ALU.subtract)
-            minus_mean[batch] = stats.tile([P, BATCH, 1], F32, name="minus_mean")
-            nc.vector.tensor_scalar(
-                out=minus_mean[batch][:], in0=both[:, :, 0:1], scalar1=-0.5, scalar2=None, op0=ALU.mult
-            )
-            gap_sq = stats.tile([P, BATCH, 1], F32, name="gap_sq")
-            nc.vector.tensor_tensor(out=gap_sq[:], in0=gap[:], in1=gap[:], op=ALU.mult)
-            within = stats.tile([P, BATCH, 1], F32, name="within")
-            nc.vector.tensor_scalar(
-                out=within[:], in0=both[:, :, 1:2], scalar1=1.0 / CHANNELS, scalar2=EPS, op0=ALU.mult, op1=ALU.add
-            )
-            var_eps = stats.tile([P, BATCH, 1], F32, name="var_eps")
-            nc.vector.scalar_tensor_tensor(
-                out=var_eps[:], in0=gap_sq[:], scalar=0.25, in1=within[:], op0=ALU.mult, op1=ALU.add
-            )
-            variance[batch] = var_eps
+                moments[batch] = stats.tile([P, BATCH, 3], F32, name="moments")
+            for j in range(0, PACK, 2):
+                first = PACK * n + j
+                nc.vector.bn_stats(
+                    out=moments[batch][:, first : first + 2, :].rearrange("p t s -> p (t s)"),
+                    in_=x_tokens(b)[:, n, g, j : j + 2, :].rearrange("p j c -> p c j"),
+                )
 
         def root(batch):
             std[batch] = stats.tile([P, BATCH, 1], F32, name="std")
-            nc.scalar.activation(out=std[batch][:], in_=variance[batch][:], func=ACT.Sqrt)
+            nc.scalar.activation(
+                out=std[batch][:],
+                in_=moments[batch][:, :, 2:3],
+                func=ACT.Sqrt,
+                scale=1.0 / CHANNELS,
+                bias=EPS,
+            )
 
         def inverse_deviation(batch):
             rstd[batch] = stats.tile([P, BATCH, 1], F32, name="rstd")
             nc.vector.reciprocal(out=rstd[batch][:], in_=std[batch][:])
+
+        def normal_shift(batch):
+            shift[batch] = stats.tile([P, BATCH, 1], F32, name="shift")
+            nc.vector.scalar_tensor_tensor(
+                out=shift[batch][:],
+                in0=moments[batch][:, :, 1:2],
+                scalar=-1.0,
+                in1=rstd[batch][:],
+                op0=ALU.mult,
+                op1=ALU.mult,
+            )
 
         x_hat = {}
         xn_turned = {}
@@ -197,10 +195,10 @@ def tile_swinmlpblocknew_pa_t_kernel(tc, x, norm1_w, norm1_b, spatial_w, spatial
                 nc.gpsimd.tensor_scalar(
                     out=x_hat[i][:, j, :],
                     in0=x_tokens(b)[:, n, g, j, :],
-                    scalar1=minus_mean[batch][:, PACK * n + j, :],
-                    scalar2=rstd[batch][:, PACK * n + j, :],
-                    op0=ALU.add,
-                    op1=ALU.mult,
+                    scalar1=rstd[batch][:, PACK * n + j, :],
+                    scalar2=shift[batch][:, PACK * n + j, :],
+                    op0=ALU.mult,
+                    op1=ALU.add,
                 )
 
         def to_channels(i):
@@ -292,6 +290,8 @@ def tile_swinmlpblocknew_pa_t_kernel(tc, x, norm1_w, norm1_b, spatial_w, spatial
                 inverse_deviation((step + STATS_LEAD - 2) // WINDOWS)
             if 0 <= step - OUT_LAG:
                 add_and_store(step - OUT_LAG)
+            if last_of_batch(step + STATS_LEAD - 2):
+                normal_shift((step + STATS_LEAD - 2) // WINDOWS)
             if last_of_batch(step - QUANT_LAG):
                 quantise_tokens((step - QUANT_LAG) // WINDOWS)
             if 0 <= step - 1 < CHUNKS:
@@ -310,8 +310,6 @@ def tile_swinmlpblocknew_pa_t_kernel(tc, x, norm1_w, norm1_b, spatial_w, spatial
                 normalise(step)
             if step + STATS_LEAD < TILES:
                 tile_statistics(step + STATS_LEAD)
-                if last_of_batch(step + STATS_LEAD):
-                    deviation((step + STATS_LEAD) // WINDOWS)
             chunk = step + LOAD_LEAD
             if 0 <= chunk < CHUNKS:
                 load_weights(chunk)

@@ -118,6 +118,7 @@ def tile_swinmlpblocknew_pa_t_kernel(tc, x, norm1_w, norm1_b, spatial_w, spatial
         w_scales = w_keep.tile([P, CHUNKS, 2 * PASSES * P], U8, name="w_scales", align_bytes=64)
         w_raw = {}
         w_grouped = {}
+        w_banks = {}
 
         def load_weights(chunk):
             kind, pair = chunk // PAIRS, chunk % PAIRS
@@ -127,15 +128,20 @@ def tile_swinmlpblocknew_pa_t_kernel(tc, x, norm1_w, norm1_b, spatial_w, spatial
             nc.sync.dma_start(out=w_raw[chunk][:], in_=rows_of_pass.rearrange("h (p j) t -> j p h t", j=PACK)[j])
 
         def turn_weights(chunk):
-            w_grouped[chunk] = w_stage.tile([P, 2 * PASSES * P * PACK], BF16, name="w_grouped", align_bytes=64)
+            w_grouped[chunk] = w_stage.tile([P, 2 * PASSES * P * PACK], BF16, name="w_grouped", bufs=3, align_bytes=64)
             words = w_raw[chunk][:].bitcast(F32).rearrange("p h (g q u) -> p h g q u", g=PASSES, u=2)
-            grouped_words = w_grouped[chunk][:].bitcast(F32).rearrange("q (h g p u) -> q h g p u", h=2, g=PASSES, u=2)
             for side in range(2):
                 bank = banks.tile([P, PASSES, 2, P], F32, tag="bank", name="w_bank")
                 for g in range(PASSES):
                     for u in range(2):
                         nc.tensor.transpose(bank[:, g, u, :], words[:, side, g, :, u], ident_f32[:])
-                nc.scalar.copy(out=grouped_words[:, side], in_=bank[:].rearrange("q g u p -> q g p u"))
+                w_banks[chunk, side] = bank
+
+        def empty_weights(engine_copy, chunk, side):
+            grouped_words = w_grouped[chunk][:].bitcast(F32).rearrange("q (h g p u) -> q h g p u", h=2, g=PASSES, u=2)
+            engine_copy(
+                out=grouped_words[:, side], in_=w_banks[chunk, side][:].rearrange("q g u p -> q g p u")
+            )
 
         def quantise_weights(chunk):
             nc.vector.quantize_mx(
@@ -295,7 +301,9 @@ def tile_swinmlpblocknew_pa_t_kernel(tc, x, norm1_w, norm1_b, spatial_w, spatial
             if last_of_batch(step - QUANT_LAG):
                 quantise_tokens((step - QUANT_LAG) // WINDOWS)
             if 0 <= step - 1 < CHUNKS:
-                quantise_weights(step - 1)
+                empty_weights(nc.vector.tensor_copy, step - 1, 1)
+            if 0 <= step - 2 < CHUNKS:
+                quantise_weights(step - 2)
             if last_of_batch(step + STATS_LEAD - 1):
                 root((step + STATS_LEAD - 1) // WINDOWS)
             if 0 <= step - BACK_LAG < TILES:
@@ -304,6 +312,7 @@ def tile_swinmlpblocknew_pa_t_kernel(tc, x, norm1_w, norm1_b, spatial_w, spatial
                 to_channels(step - TURN_LAG)
             if 0 <= step < CHUNKS:
                 turn_weights(step)
+                empty_weights(nc.scalar.copy, step, 0)
             if 0 <= step - MIX_LAG < UNITS:
                 multiply(step - MIX_LAG)
             if 0 <= step < TILES:

@@ -23,23 +23,26 @@ HEADS = 4
 HEAD_DIM = CHANNELS // HEADS
 EPS = 1e-5
 COLS = WINDOWS * HEAD_DIM
-BATCH = WINDOWS * PACK
-TILES_PER_IMAGE = PASSES * WINDOWS
+RUN = TOKENS // P
+BATCH = 2 * RUN
+GROUPS = 4
+TILES_PER_IMAGE = 2 * WINDOWS
 TILES = IMAGES * TILES_PER_IMAGE
-UNITS = TILES
-KINDS = PASSES * PACK
+TILES_PER_BATCH = 4
+UNITS = IMAGES * RUN
 PAIRS = HEADS // 2
-CHUNKS = KINDS * PAIRS
+CHUNKS = RUN * PAIRS
+STORE = 4
 PSUM_BANKS = 8
 
-STATS_LEAD = 8
+STATS_LEAD = 6
 TURN_LAG = 1
 BACK_LAG = 3
 QUANT_LAG = BACK_LAG + 1
 MIX_LAG = TILES_PER_IMAGE - 1 + QUANT_LAG + 1
 OUT_LAG = MIX_LAG + 1
 LOAD_LEAD = 4
-TILES_PER_LOAD = 2
+LOADS_PER_CHUNK = 2
 
 FLOPS = 2 * IMAGES * WINDOWS * HEADS * TOKENS * TOKENS * HEAD_DIM
 
@@ -47,10 +50,10 @@ FLOPS = 2 * IMAGES * WINDOWS * HEADS * TOKENS * TOKENS * HEAD_DIM
 def tile_swinmlpblocknew_pa_t_kernel(tc, x, norm1_w, norm1_b, spatial_w, spatial_b, out):
     nc = tc.nc
 
-    cut = "b (wr g r wc q j) c -> b wr wc g r q (j c)"
-    sizes = dict(wr=2, g=PASSES, r=16, wc=2, q=8, j=PACK)
-    x_cut = x.rearrange(cut, **sizes)
-    out_cut = out.rearrange(cut, **sizes)
+    x_cut = x.rearrange("b (wr r wc cg j) c -> b wc cg r wr (j c)", wr=2, r=32, wc=2, cg=GROUPS, j=RUN)
+    out_cut = out.rearrange(
+        "b (wr r wc cg k j) c -> b wc cg k r wr (j c)", wr=2, r=32, wc=2, cg=GROUPS, k=RUN // STORE, j=STORE
+    )
 
     with ExitStack() as ctx:
         const = ctx.enter_context(tc.tile_pool(name="const", bufs=1))
@@ -59,60 +62,63 @@ def tile_swinmlpblocknew_pa_t_kernel(tc, x, norm1_w, norm1_b, spatial_w, spatial
         w_stage = ctx.enter_context(tc.tile_pool(name="w_stage", bufs=2))
         stats = ctx.enter_context(tc.tile_pool(name="stats", bufs=4))
         norm = ctx.enter_context(tc.tile_pool(name="norm", bufs=3))
-        x_stage = ctx.enter_context(tc.tile_pool(name="x_stage", bufs=2))
+        x_stage = ctx.enter_context(tc.tile_pool(name="x_stage", bufs=3))
         x_keep = ctx.enter_context(tc.tile_pool(name="x_keep", bufs=2 * PASSES))
         results = ctx.enter_context(tc.tile_pool(name="results", bufs=2))
         banks = ctx.enter_context(tc.psum_pool(name="banks", bufs=PSUM_BANKS))
         ctx.enter_context(tc.manual_schedule())
 
         def place(i):
-            batch, n = i // WINDOWS, i % WINDOWS
-            return batch, batch // PASSES, batch % PASSES, n
+            return i // TILES_PER_IMAGE, (i // 2) % WINDOWS, i % 2
 
-        x_sb = [images.tile([P, TILES_PER_IMAGE * PACK * CHANNELS], BF16, name="x_sb%d" % b) for b in range(IMAGES)]
+        x_sb = [images.tile([P, WINDOWS * RUN * CHANNELS], BF16, name="x_sb%d" % b) for b in range(IMAGES)]
 
         def x_tokens(b):
-            return x_sb[b][:].rearrange("p (n g j c) -> p n g j c", n=WINDOWS, g=PASSES, j=PACK)
+            return x_sb[b][:].rearrange("p (n j c) -> p n j c", n=WINDOWS, j=RUN)
 
-        def load_tile(i):
-            batch, b, g, n = place(i)
-            rows = x_sb[b][:].rearrange("p (n g f) -> p n g f", n=WINDOWS, g=PASSES)
-            nc.sync.dma_start(out=rows[:, n, g, :], in_=x_cut[b, n // 2, n % 2, g])
+        def load_window(b, n, cg):
+            rows = x_sb[b][:].rearrange("p (n f) -> p n f", n=WINDOWS)
+            nc.sync.dma_start(out=rows[cg:P:GROUPS, n, :], in_=x_cut[b, n // 2, cg][:, n % 2, :])
 
-        for i in range(TILES_PER_IMAGE):
-            load_tile(i)
+        def load_two_windows(b, wc, cg):
+            rows = x_sb[b][:].rearrange("p (n f) -> p n f", n=WINDOWS)
+            nc.sync.dma_start(out=rows[cg:P:GROUPS, 2 * wc : 2 * wc + 2, :], in_=x_cut[b, wc, cg])
 
+        bias_rows = const.tile([P, TOKENS], BF16, name="bias_rows")
+        nc.scalar.dma_start(out=bias_rows[0:HEADS, :], in_=spatial_b)
+        rows = const.tile([P, RUN, P], BF16, name="rows")
+        nc.gpsimd.memset(rows[:], 0.0)
+        gain_row, shift_row = HEADS, HEADS + HALVES
+        nc.scalar.dma_start(
+            out=rows[gain_row : gain_row + HALVES, 0, :], in_=norm1_w.rearrange("(a c) -> a c", a=HALVES)
+        )
+        nc.scalar.dma_start(
+            out=rows[shift_row : shift_row + HALVES, 0, :], in_=norm1_b.rearrange("(a c) -> a c", a=HALVES)
+        )
+        for n in range(WINDOWS):
+            for cg in range(GROUPS):
+                load_window(0, n, cg)
         ident_f32 = const.tile([P, P], F32, name="ident_f32")
         make_identity(nc, ident_f32[:])
         ident_bf16 = const.tile([P, P], BF16, name="ident_bf16")
         make_identity(nc, ident_bf16[:])
-
-        bias_rows = const.tile([P, P * PACK], BF16, name="bias_rows")
-        nc.scalar.dma_start(
-            out=bias_rows[0 : HEADS * PASSES, :], in_=spatial_b.rearrange("h (g f) -> (h g) f", g=PASSES)
-        )
-        rows = const.tile([P, PACK + 1, P], BF16, name="rows")
-        nc.gpsimd.memset(rows[:], 0.0)
-        nc.scalar.dma_start(out=rows[0:HALVES, PACK, :], in_=norm1_w.rearrange("(a c) -> a c", a=HALVES))
-        nc.scalar.dma_start(out=rows[HALVES : 2 * HALVES, PACK, :], in_=norm1_b.rearrange("(a c) -> a c", a=HALVES))
         nc.gpsimd.tensor_copy(
-            out=rows[0 : HEADS * PASSES, 0:PACK, :],
-            in_=bias_rows[0 : HEADS * PASSES, :].rearrange("r (p j) -> r j p", j=PACK),
+            out=rows[0:HEADS, :, :], in_=bias_rows[0:HEADS, :].rearrange("h (p j) -> h j p", j=RUN)
         )
-        rows_turned = banks.tile([P, 8, P], BF16, tag="bank", name="rows_turned")
-        for plane in range(PACK + 1):
+        rows_turned = banks.tile([P, RUN, P], BF16, tag="bank", name="rows_turned")
+        for plane in range(RUN):
             nc.tensor.transpose(rows_turned[:, plane, :], rows[:, plane, :], ident_bf16[:])
-        columns = const.tile([P, PACK + 1, HEADS * PASSES], F32, name="columns")
-        nc.scalar.copy(out=columns[:], in_=rows_turned[:, 0 : PACK + 1, 0 : HEADS * PASSES])
+        columns = const.tile([P, RUN, HEADS + 2 * HALVES], F32, name="columns")
+        nc.scalar.copy(out=columns[:], in_=rows_turned[:, :, 0 : HEADS + 2 * HALVES])
 
-        def bias_column(h, g, j):
-            return columns[:, j, PASSES * h + g : PASSES * h + g + 1]
+        def bias_column(h, j):
+            return columns[:, j, h : h + 1]
 
         def gain_column(half):
-            return columns[:, PACK, half : half + 1]
+            return columns[:, 0, gain_row + half : gain_row + half + 1]
 
         def shift_column(half):
-            return columns[:, PACK, HALVES + half : HALVES + half + 1]
+            return columns[:, 0, shift_row + half : shift_row + half + 1]
 
         w_codes = w_keep.tile([P, CHUNKS, 2 * PASSES * P], U32, name="w_codes", align_bytes=64)
         w_scales = w_keep.tile([P, CHUNKS, 2 * PASSES * P], U8, name="w_scales", align_bytes=64)
@@ -121,11 +127,10 @@ def tile_swinmlpblocknew_pa_t_kernel(tc, x, norm1_w, norm1_b, spatial_w, spatial
         w_banks = {}
 
         def load_weights(chunk):
-            kind, pair = chunk // PAIRS, chunk % PAIRS
-            g_out, j = kind // PACK, kind % PACK
+            j, pair = chunk // PAIRS, chunk % PAIRS
             w_raw[chunk] = w_stage.tile([P, 2, TOKENS], BF16, name="w_raw", bufs=LOAD_LEAD)
-            rows_of_pass = spatial_w[2 * pair : 2 * pair + 2, g_out * P * PACK : (g_out + 1) * P * PACK, :]
-            nc.sync.dma_start(out=w_raw[chunk][:], in_=rows_of_pass.rearrange("h (p j) t -> j p h t", j=PACK)[j])
+            heads = spatial_w[2 * pair : 2 * pair + 2]
+            nc.sync.dma_start(out=w_raw[chunk][:], in_=heads.rearrange("h (p j) t -> j p h t", j=RUN)[j])
 
         def turn_weights(chunk):
             w_grouped[chunk] = w_stage.tile([P, 2 * PASSES * P * PACK], BF16, name="w_grouped", bufs=3, align_bytes=64)
@@ -153,15 +158,18 @@ def tile_swinmlpblocknew_pa_t_kernel(tc, x, norm1_w, norm1_b, spatial_w, spatial
         rstd = {}
         shift = {}
 
+        def slot(i, j):
+            return (i // 2 % 2) * RUN + j
+
         def tile_statistics(i):
-            batch, b, g, n = place(i)
-            if n == 0:
+            b, n, u = place(i)
+            batch = i // TILES_PER_BATCH
+            if i % TILES_PER_BATCH == 0:
                 moments[batch] = stats.tile([P, BATCH, 3], F32, name="moments")
-            for j in range(0, PACK, 2):
-                first = PACK * n + j
+            for j in (2 * u, 2 * u + 4):
                 nc.vector.bn_stats(
-                    out=moments[batch][:, first : first + 2, :].rearrange("p t s -> p (t s)"),
-                    in_=x_tokens(b)[:, n, g, j : j + 2, :].rearrange("p j c -> p c j"),
+                    out=moments[batch][:, slot(i, j) : slot(i, j) + 2, :].rearrange("p t s -> p (t s)"),
+                    in_=x_tokens(b)[:, n, j : j + 2, :].rearrange("p j c -> p c j"),
                 )
 
         def root(batch):
@@ -195,65 +203,69 @@ def tile_swinmlpblocknew_pa_t_kernel(tc, x, norm1_w, norm1_b, spatial_w, spatial
         x_codes = {}
 
         def normalise(i):
-            batch, b, g, n = place(i)
+            b, n, u = place(i)
+            batch = i // TILES_PER_BATCH
             x_hat[i] = norm.tile([P, PACK, CHANNELS], F32, name="x_hat")
-            for j in range(PACK):
+            for k, j in enumerate((2 * u, 2 * u + 1, 2 * u + 4, 2 * u + 5)):
                 nc.gpsimd.tensor_scalar(
-                    out=x_hat[i][:, j, :],
-                    in0=x_tokens(b)[:, n, g, j, :],
-                    scalar1=rstd[batch][:, PACK * n + j, :],
-                    scalar2=shift[batch][:, PACK * n + j, :],
+                    out=x_hat[i][:, k, :],
+                    in0=x_tokens(b)[:, n, j, :],
+                    scalar1=rstd[batch][:, slot(i, j), :],
+                    scalar2=shift[batch][:, slot(i, j), :],
                     op0=ALU.mult,
                     op1=ALU.add,
                 )
 
         def to_channels(i):
-            xn_turned[i] = norm.tile([P, HALVES, 2, P, 2], BF16, name="xn_turned")
+            u = i % 2
+            if u == 0:
+                xn_turned[i // 2] = norm.tile([P, HALVES, 2, P, 2, 2], BF16, name="xn_turned", bufs=2)
             for half in range(HALVES):
                 bank = banks.tile([P, PACK, P], F32, tag="bank", name="hat_bank")
-                for j in range(PACK):
-                    nc.tensor.transpose(bank[:, j, :], x_hat[i][:, j, half * P : (half + 1) * P], ident_f32[:])
+                for k in range(PACK):
+                    nc.tensor.transpose(bank[:, k, :], x_hat[i][:, k, half * P : (half + 1) * P], ident_f32[:])
                 nc.scalar.activation(
-                    out=xn_turned[i][:, half],
-                    in_=bank[:].rearrange("c (u e) p -> c u p e", u=2),
+                    out=xn_turned[i // 2][:, half, u],
+                    in_=bank[:].rearrange("c (jh e) p -> c p jh e", jh=2),
                     func=ACT.Identity,
                     bias=shift_column(half),
                     scale=gain_column(half),
                 )
 
         def to_tokens(i):
-            batch, b, g, n = place(i)
-            words = xn_turned[i][:].rearrange("c a u p e -> c (a u p e)").bitcast(F32)
-            words = words.rearrange("c (a u q) -> c a u q", a=HALVES, u=2)
+            b, n, g = place(i)
+            words = xn_turned[i // 2][:].rearrange("c a u p jh e -> c (a u p jh e)").bitcast(F32)
+            words = words.rearrange("c (a u g q) -> c a u g q", a=HALVES, u=2, g=PASSES)
             bank = banks.tile([P, 2, CHANNELS], F32, tag="bank", name="xn_bank")
             for u in range(2):
                 for half in range(HALVES):
-                    nc.tensor.transpose(bank[:, u, half * P : (half + 1) * P], words[:, half, u, :], ident_f32[:])
+                    nc.tensor.transpose(bank[:, u, half * P : (half + 1) * P], words[:, half, u, g, :], ident_f32[:])
             if n == 0:
-                x_grouped[batch] = x_stage.tile([P, HEADS * COLS * PACK], BF16, name="x_grouped", align_bytes=64)
+                x_grouped[b, g] = x_stage.tile([P, HEADS * COLS * PACK], BF16, name="x_grouped", align_bytes=64)
             grouped_words = (
-                x_grouped[batch][:].bitcast(F32).rearrange("q (h n d u) -> q h n d u", h=HEADS, n=WINDOWS, u=2)
+                x_grouped[b, g][:].bitcast(F32).rearrange("q (h n d u) -> q h n d u", h=HEADS, n=WINDOWS, u=2)
             )
             nc.scalar.copy(out=grouped_words[:, :, n], in_=bank[:].rearrange("q u (h d) -> q h d u", h=HEADS))
 
-        def quantise_tokens(batch):
+        def quantise_tokens(i):
+            b, n, g = place(i)
             codes = x_keep.tile([P, HEADS * COLS], U32, name="x_codes", align_bytes=64)
             scales = x_keep.tile([P, HEADS * COLS], U8, name="x_scales", align_bytes=64)
-            nc.vector.quantize_mx(out=codes[:].bitcast(FP8X4), scales=scales[:], in_=x_grouped[batch][:])
-            x_codes[batch] = (codes, scales)
+            nc.vector.quantize_mx(out=codes[:].bitcast(FP8X4), scales=scales[:], in_=x_grouped[b, g][:])
+            x_codes[b, g] = (codes, scales)
 
         sums = {}
         result = {}
 
         def multiply(unit):
-            b, kind = unit // KINDS, unit % KINDS
+            b, j = unit // RUN, unit % RUN
             for pair in range(PAIRS):
-                chunk = PAIRS * kind + pair
+                chunk = PAIRS * j + pair
                 sums[unit, pair] = banks.tile([P, 2, COLS], F32, tag="bank", name="sum_bank")
                 for side in range(2):
                     h = 2 * pair + side
                     for g in range(PASSES):
-                        codes, scales = x_codes[PASSES * b + g]
+                        codes, scales = x_codes[b, g]
                         w_cols = slice((PASSES * side + g) * P, (PASSES * side + g + 1) * P)
                         x_cols = slice(h * COLS, (h + 1) * COLS)
                         nc.tensor.matmul_mx(
@@ -267,45 +279,50 @@ def tile_swinmlpblocknew_pa_t_kernel(tc, x, norm1_w, norm1_b, spatial_w, spatial
                         )
 
         def add_and_store(unit):
-            b, kind = unit // KINDS, unit % KINDS
-            g_out, j = kind // PACK, kind % PACK
-            if j == 0:
-                result[b, g_out] = results.tile([P, WINDOWS, PACK, CHANNELS], F32, name="result")
-            res = result[b, g_out]
+            b, j = unit // RUN, unit % RUN
+            k = j % STORE
+            if k == 0:
+                result[unit // STORE] = results.tile([P, WINDOWS, STORE, CHANNELS], F32, name="result")
+            res = result[unit // STORE]
             for h in range(HEADS):
                 channels = slice(h * HEAD_DIM, (h + 1) * HEAD_DIM)
                 nc.vector.scalar_tensor_tensor(
-                    out=res[:, :, j, channels],
+                    out=res[:, :, k, channels],
                     in0=sums[unit, h // 2][:, h % 2, :].rearrange("p (n d) -> p n d", n=WINDOWS),
-                    scalar=bias_column(h, g_out, j),
-                    in1=x_tokens(b)[:, :, g_out, j, channels],
+                    scalar=bias_column(h, j),
+                    in1=x_tokens(b)[:, :, j, channels],
                     op0=ALU.add,
                     op1=ALU.add,
                 )
-            if j == PACK - 1:
-                for n in range(WINDOWS):
-                    nc.sync.dma_start(
-                        out=out_cut[b, n // 2, n % 2, g_out], in_=res[:, n].rearrange("p j c -> p (j c)")
-                    )
+            if k == STORE - 1:
+                runs = res[:].rearrange("p n k c -> p n (k c)")
+                for wc in range(2):
+                    for cg in range(GROUPS):
+                        nc.sync.dma_start(
+                            out=out_cut[b, wc, cg, j // STORE], in_=runs[cg:P:GROUPS, 2 * wc : 2 * wc + 2, :]
+                        )
 
         def last_of_batch(i):
-            return 0 <= i < TILES and i % WINDOWS == WINDOWS - 1
+            return 0 <= i < TILES and i % TILES_PER_BATCH == TILES_PER_BATCH - 1
+
+        def last_window(i):
+            return 0 <= i < TILES and place(i)[1] == WINDOWS - 1
 
         for step in range(-STATS_LEAD, UNITS + OUT_LAG):
             if last_of_batch(step + STATS_LEAD - 2):
-                inverse_deviation((step + STATS_LEAD - 2) // WINDOWS)
+                inverse_deviation((step + STATS_LEAD - 2) // TILES_PER_BATCH)
             if 0 <= step - OUT_LAG:
                 add_and_store(step - OUT_LAG)
             if last_of_batch(step + STATS_LEAD - 2):
-                normal_shift((step + STATS_LEAD - 2) // WINDOWS)
-            if last_of_batch(step - QUANT_LAG):
-                quantise_tokens((step - QUANT_LAG) // WINDOWS)
+                normal_shift((step + STATS_LEAD - 2) // TILES_PER_BATCH)
+            if last_window(step - QUANT_LAG):
+                quantise_tokens(step - QUANT_LAG)
             if 0 <= step - 1 < CHUNKS:
                 empty_weights(nc.vector.tensor_copy, step - 1, 1)
             if 0 <= step - 2 < CHUNKS:
                 quantise_weights(step - 2)
             if last_of_batch(step + STATS_LEAD - 1):
-                root((step + STATS_LEAD - 1) // WINDOWS)
+                root((step + STATS_LEAD - 1) // TILES_PER_BATCH)
             if 0 <= step - BACK_LAG < TILES:
                 to_tokens(step - BACK_LAG)
             if 0 <= step - TURN_LAG < TILES:
@@ -322,6 +339,6 @@ def tile_swinmlpblocknew_pa_t_kernel(tc, x, norm1_w, norm1_b, spatial_w, spatial
             chunk = step + LOAD_LEAD
             if 0 <= chunk < CHUNKS:
                 load_weights(chunk)
-                first = TILES_PER_IMAGE + TILES_PER_LOAD * chunk
-                for i in range(first, min(first + TILES_PER_LOAD, TILES)):
-                    load_tile(i)
+                first = LOADS_PER_CHUNK * chunk
+                for i in range(first, min(first + LOADS_PER_CHUNK, (IMAGES - 1) * 2 * GROUPS)):
+                    load_two_windows(1 + i // (2 * GROUPS), i // GROUPS % 2, i % GROUPS)

@@ -24,25 +24,22 @@ HEAD_DIM = CHANNELS // HEADS
 EPS = 1e-5
 COLS = WINDOWS * HEAD_DIM
 RUN = TOKENS // P
-BATCH = 2 * RUN
 GROUPS = 4
 TILES_PER_IMAGE = 2 * WINDOWS
 TILES = IMAGES * TILES_PER_IMAGE
-TILES_PER_BATCH = 4
 UNITS = IMAGES * RUN
 PAIRS = HEADS // 2
 CHUNKS = RUN * PAIRS
-STORE = 4
+STORE = 2
 PSUM_BANKS = 8
 
-STATS_LEAD = 6
+STATS_LEAD = 3
 TURN_LAG = 1
 BACK_LAG = 3
 QUANT_LAG = BACK_LAG + 1
 MIX_LAG = TILES_PER_IMAGE - 1 + QUANT_LAG + 1
 OUT_LAG = MIX_LAG + 1
 LOAD_LEAD = 4
-LOADS_PER_CHUNK = 2
 
 FLOPS = 2 * IMAGES * WINDOWS * HEADS * TOKENS * TOKENS * HEAD_DIM
 
@@ -60,11 +57,11 @@ def tile_swinmlpblocknew_pa_t_kernel(tc, x, norm1_w, norm1_b, spatial_w, spatial
         images = ctx.enter_context(tc.tile_pool(name="images", bufs=1))
         w_keep = ctx.enter_context(tc.tile_pool(name="w_keep", bufs=1))
         w_stage = ctx.enter_context(tc.tile_pool(name="w_stage", bufs=2))
-        stats = ctx.enter_context(tc.tile_pool(name="stats", bufs=4))
+        stats = ctx.enter_context(tc.tile_pool(name="stats", bufs=IMAGES * WINDOWS))
         norm = ctx.enter_context(tc.tile_pool(name="norm", bufs=3))
         x_stage = ctx.enter_context(tc.tile_pool(name="x_stage", bufs=3))
         x_keep = ctx.enter_context(tc.tile_pool(name="x_keep", bufs=2 * PASSES))
-        results = ctx.enter_context(tc.tile_pool(name="results", bufs=2))
+        results = ctx.enter_context(tc.tile_pool(name="results", bufs=4))
         banks = ctx.enter_context(tc.psum_pool(name="banks", bufs=PSUM_BANKS))
         ctx.enter_context(tc.manual_schedule())
 
@@ -76,13 +73,10 @@ def tile_swinmlpblocknew_pa_t_kernel(tc, x, norm1_w, norm1_b, spatial_w, spatial
         def x_tokens(b):
             return x_sb[b][:].rearrange("p (n j c) -> p n j c", n=WINDOWS, j=RUN)
 
-        def load_window(b, n, cg):
+        def load_window(b, n):
             rows = x_sb[b][:].rearrange("p (n f) -> p n f", n=WINDOWS)
-            nc.sync.dma_start(out=rows[cg:P:GROUPS, n, :], in_=x_cut[b, n // 2, cg][:, n % 2, :])
-
-        def load_two_windows(b, wc, cg):
-            rows = x_sb[b][:].rearrange("p (n f) -> p n f", n=WINDOWS)
-            nc.sync.dma_start(out=rows[cg:P:GROUPS, 2 * wc : 2 * wc + 2, :], in_=x_cut[b, wc, cg])
+            for cg in range(GROUPS):
+                nc.sync.dma_start(out=rows[cg:P:GROUPS, n, :], in_=x_cut[b, n // 2, cg][:, n % 2, :])
 
         bias_rows = const.tile([P, TOKENS], BF16, name="bias_rows")
         nc.scalar.dma_start(out=bias_rows[0:HEADS, :], in_=spatial_b)
@@ -95,9 +89,6 @@ def tile_swinmlpblocknew_pa_t_kernel(tc, x, norm1_w, norm1_b, spatial_w, spatial
         nc.scalar.dma_start(
             out=rows[shift_row : shift_row + HALVES, 0, :], in_=norm1_b.rearrange("(a c) -> a c", a=HALVES)
         )
-        for n in range(WINDOWS):
-            for cg in range(GROUPS):
-                load_window(0, n, cg)
         ident_f32 = const.tile([P, P], F32, name="ident_f32")
         make_identity(nc, ident_f32[:])
         ident_bf16 = const.tile([P, P], BF16, name="ident_bf16")
@@ -153,46 +144,48 @@ def tile_swinmlpblocknew_pa_t_kernel(tc, x, norm1_w, norm1_b, spatial_w, spatial
                 out=w_codes[:, chunk, :].bitcast(FP8X4), scales=w_scales[:, chunk, :], in_=w_grouped[chunk][:]
             )
 
+        for n in range(WINDOWS):
+            load_window(0, n)
+            if n == 1:
+                load_weights(0)
+
         moments = {}
         std = {}
         rstd = {}
         shift = {}
 
-        def slot(i, j):
-            return (i // 2 % 2) * RUN + j
-
         def tile_statistics(i):
             b, n, u = place(i)
-            batch = i // TILES_PER_BATCH
-            if i % TILES_PER_BATCH == 0:
-                moments[batch] = stats.tile([P, BATCH, 3], F32, name="moments")
+            window = i // 2
+            if u == 0:
+                moments[window] = stats.tile([P, RUN, 3], F32, name="moments")
             for j in (2 * u, 2 * u + 4):
                 nc.vector.bn_stats(
-                    out=moments[batch][:, slot(i, j) : slot(i, j) + 2, :].rearrange("p t s -> p (t s)"),
+                    out=moments[window][:, j : j + 2, :].rearrange("p t s -> p (t s)"),
                     in_=x_tokens(b)[:, n, j : j + 2, :].rearrange("p j c -> p c j"),
                 )
 
-        def root(batch):
-            std[batch] = stats.tile([P, BATCH, 1], F32, name="std")
+        def root(window):
+            std[window] = stats.tile([P, RUN, 1], F32, name="std")
             nc.scalar.activation(
-                out=std[batch][:],
-                in_=moments[batch][:, :, 2:3],
+                out=std[window][:],
+                in_=moments[window][:, :, 2:3],
                 func=ACT.Sqrt,
                 scale=1.0 / CHANNELS,
                 bias=EPS,
             )
 
-        def inverse_deviation(batch):
-            rstd[batch] = stats.tile([P, BATCH, 1], F32, name="rstd")
-            nc.vector.reciprocal(out=rstd[batch][:], in_=std[batch][:])
+        def inverse_deviation(window):
+            rstd[window] = stats.tile([P, RUN, 1], F32, name="rstd")
+            nc.vector.reciprocal(out=rstd[window][:], in_=std[window][:])
 
-        def normal_shift(batch):
-            shift[batch] = stats.tile([P, BATCH, 1], F32, name="shift")
+        def normal_shift(window):
+            shift[window] = stats.tile([P, RUN, 1], F32, name="shift")
             nc.vector.scalar_tensor_tensor(
-                out=shift[batch][:],
-                in0=moments[batch][:, :, 1:2],
+                out=shift[window][:],
+                in0=moments[window][:, :, 1:2],
                 scalar=-1.0,
-                in1=rstd[batch][:],
+                in1=rstd[window][:],
                 op0=ALU.mult,
                 op1=ALU.mult,
             )
@@ -204,14 +197,14 @@ def tile_swinmlpblocknew_pa_t_kernel(tc, x, norm1_w, norm1_b, spatial_w, spatial
 
         def normalise(i):
             b, n, u = place(i)
-            batch = i // TILES_PER_BATCH
+            window = i // 2
             x_hat[i] = norm.tile([P, PACK, CHANNELS], F32, name="x_hat")
             for k, j in enumerate((2 * u, 2 * u + 1, 2 * u + 4, 2 * u + 5)):
                 nc.gpsimd.tensor_scalar(
                     out=x_hat[i][:, k, :],
                     in0=x_tokens(b)[:, n, j, :],
-                    scalar1=rstd[batch][:, slot(i, j), :],
-                    scalar2=shift[batch][:, slot(i, j), :],
+                    scalar1=rstd[window][:, j, :],
+                    scalar2=shift[window][:, j, :],
                     op0=ALU.mult,
                     op1=ALU.add,
                 )
@@ -302,27 +295,26 @@ def tile_swinmlpblocknew_pa_t_kernel(tc, x, norm1_w, norm1_b, spatial_w, spatial
                             out=out_cut[b, wc, cg, j // STORE], in_=runs[cg:P:GROUPS, 2 * wc : 2 * wc + 2, :]
                         )
 
-        def last_of_batch(i):
-            return 0 <= i < TILES and i % TILES_PER_BATCH == TILES_PER_BATCH - 1
+        def tiles_of_statistics(step):
+            return [i for i in range(TILES) if 3 * i // 4 - STATS_LEAD == step]
+
+        def finished_windows(step):
+            return [i // 2 for i in tiles_of_statistics(step) if i % 2 == 1]
 
         def last_window(i):
             return 0 <= i < TILES and place(i)[1] == WINDOWS - 1
 
-        for step in range(-STATS_LEAD, UNITS + OUT_LAG):
-            if last_of_batch(step + STATS_LEAD - 2):
-                inverse_deviation((step + STATS_LEAD - 2) // TILES_PER_BATCH)
+        for step in range(-LOAD_LEAD, UNITS + OUT_LAG):
+            for window in finished_windows(step - 2):
+                inverse_deviation(window)
             if 0 <= step - OUT_LAG:
                 add_and_store(step - OUT_LAG)
-            if last_of_batch(step + STATS_LEAD - 2):
-                normal_shift((step + STATS_LEAD - 2) // TILES_PER_BATCH)
             if last_window(step - QUANT_LAG):
                 quantise_tokens(step - QUANT_LAG)
             if 0 <= step - 1 < CHUNKS:
-                empty_weights(nc.vector.tensor_copy, step - 1, 1)
-            if 0 <= step - 2 < CHUNKS:
-                quantise_weights(step - 2)
-            if last_of_batch(step + STATS_LEAD - 1):
-                root((step + STATS_LEAD - 1) // TILES_PER_BATCH)
+                quantise_weights(step - 1)
+            for window in finished_windows(step - 1):
+                root(window)
             if 0 <= step - BACK_LAG < TILES:
                 to_tokens(step - BACK_LAG)
             if 0 <= step - TURN_LAG < TILES:
@@ -330,15 +322,17 @@ def tile_swinmlpblocknew_pa_t_kernel(tc, x, norm1_w, norm1_b, spatial_w, spatial
             if 0 <= step < CHUNKS:
                 turn_weights(step)
                 empty_weights(nc.scalar.copy, step, 0)
+                empty_weights(nc.scalar.copy, step, 1)
             if 0 <= step - MIX_LAG < UNITS:
                 multiply(step - MIX_LAG)
             if 0 <= step < TILES:
                 normalise(step)
-            if step + STATS_LEAD < TILES:
-                tile_statistics(step + STATS_LEAD)
+            for window in finished_windows(step - 2):
+                normal_shift(window)
+            for i in tiles_of_statistics(step):
+                tile_statistics(i)
             chunk = step + LOAD_LEAD
-            if 0 <= chunk < CHUNKS:
+            if 1 <= chunk < CHUNKS:
                 load_weights(chunk)
-                first = LOADS_PER_CHUNK * chunk
-                for i in range(first, min(first + LOADS_PER_CHUNK, (IMAGES - 1) * 2 * GROUPS)):
-                    load_two_windows(1 + i // (2 * GROUPS), i // GROUPS % 2, i % GROUPS)
+            if 0 <= chunk < (IMAGES - 1) * WINDOWS:
+                load_window(1 + chunk // WINDOWS, chunk % WINDOWS)

@@ -200,14 +200,23 @@ def tile_swinmlpblocknew_pa_t_kernel(tc, x, norm1_w, norm1_b, spatial_w, spatial
             window = i // 2
             x_hat[i] = norm.tile([P, PACK, CHANNELS], F32, name="x_hat")
             for k, j in enumerate((2 * u, 2 * u + 1, 2 * u + 4, 2 * u + 5)):
-                nc.gpsimd.tensor_scalar(
-                    out=x_hat[i][:, k, :],
-                    in0=x_tokens(b)[:, n, j, :],
-                    scalar1=rstd[window][:, j, :],
-                    scalar2=shift[window][:, j, :],
-                    op0=ALU.mult,
-                    op1=ALU.add,
-                )
+                if k == PACK - 1:
+                    nc.scalar.activation(
+                        out=x_hat[i][:, k, :],
+                        in_=x_tokens(b)[:, n, j, :],
+                        func=ACT.Identity,
+                        scale=rstd[window][:, j, :],
+                        bias=shift[window][:, j, :],
+                    )
+                else:
+                    nc.gpsimd.tensor_scalar(
+                        out=x_hat[i][:, k, :],
+                        in0=x_tokens(b)[:, n, j, :],
+                        scalar1=rstd[window][:, j, :],
+                        scalar2=shift[window][:, j, :],
+                        op0=ALU.mult,
+                        op1=ALU.add,
+                    )
 
         def to_channels(i):
             u = i % 2
@@ -312,7 +321,9 @@ def tile_swinmlpblocknew_pa_t_kernel(tc, x, norm1_w, norm1_b, spatial_w, spatial
             if last_window(step - QUANT_LAG):
                 quantise_tokens(step - QUANT_LAG)
             if 0 <= step - 1 < CHUNKS:
-                quantise_weights(step - 1)
+                empty_weights(nc.vector.tensor_copy, step - 1, 1)
+            if 0 <= step - 2 < CHUNKS:
+                quantise_weights(step - 2)
             for window in finished_windows(step - 1):
                 root(window)
             if 0 <= step - BACK_LAG < TILES:
@@ -322,7 +333,6 @@ def tile_swinmlpblocknew_pa_t_kernel(tc, x, norm1_w, norm1_b, spatial_w, spatial
             if 0 <= step < CHUNKS:
                 turn_weights(step)
                 empty_weights(nc.scalar.copy, step, 0)
-                empty_weights(nc.scalar.copy, step, 1)
             if 0 <= step - MIX_LAG < UNITS:
                 multiply(step - MIX_LAG)
             if 0 <= step < TILES:

@@ -35,7 +35,7 @@ PSUM_BANKS = 8
 
 STATS_LEAD = 3
 TURN_LAG = 1
-BACK_LAG = 3
+BACK_LAG = 4
 QUANT_LAG = BACK_LAG + 1
 MIX_LAG = TILES_PER_IMAGE - 1 + QUANT_LAG + 1
 OUT_LAG = MIX_LAG + 1
@@ -57,7 +57,7 @@ def tile_swinmlpblocknew_pa_t_kernel(tc, x, norm1_w, norm1_b, spatial_w, spatial
         images = ctx.enter_context(tc.tile_pool(name="images", bufs=1))
         w_keep = ctx.enter_context(tc.tile_pool(name="w_keep", bufs=1))
         w_stage = ctx.enter_context(tc.tile_pool(name="w_stage", bufs=2))
-        stats = ctx.enter_context(tc.tile_pool(name="stats", bufs=IMAGES * WINDOWS))
+        stats = ctx.enter_context(tc.tile_pool(name="stats", bufs=2 * WINDOWS))
         norm = ctx.enter_context(tc.tile_pool(name="norm", bufs=3))
         x_stage = ctx.enter_context(tc.tile_pool(name="x_stage", bufs=3))
         x_keep = ctx.enter_context(tc.tile_pool(name="x_keep", bufs=2 * PASSES))
@@ -195,33 +195,26 @@ def tile_swinmlpblocknew_pa_t_kernel(tc, x, norm1_w, norm1_b, spatial_w, spatial
         x_grouped = {}
         x_codes = {}
 
-        def normalise(i):
+        def normalise(i, places):
             b, n, u = place(i)
             window = i // 2
-            x_hat[i] = norm.tile([P, PACK, CHANNELS], F32, name="x_hat")
-            for k, j in enumerate((2 * u, 2 * u + 1, 2 * u + 4, 2 * u + 5)):
+            if i not in x_hat:
+                x_hat[i] = norm.tile([P, PACK, CHANNELS], F32, name="x_hat")
+            for k in places:
+                j = (2 * u, 2 * u + 1, 2 * u + 4, 2 * u + 5)[k]
+                token, normal = x_tokens(b)[:, n, j, :], x_hat[i][:, k, :]
+                scale, bias = rstd[window][:, j, :], shift[window][:, j, :]
                 if k == PACK - 1:
-                    nc.scalar.activation(
-                        out=x_hat[i][:, k, :],
-                        in_=x_tokens(b)[:, n, j, :],
-                        func=ACT.Identity,
-                        scale=rstd[window][:, j, :],
-                        bias=shift[window][:, j, :],
-                    )
+                    nc.scalar.activation(out=normal, in_=token, func=ACT.Identity, scale=scale, bias=bias)
                 else:
                     nc.gpsimd.tensor_scalar(
-                        out=x_hat[i][:, k, :],
-                        in0=x_tokens(b)[:, n, j, :],
-                        scalar1=rstd[window][:, j, :],
-                        scalar2=shift[window][:, j, :],
-                        op0=ALU.mult,
-                        op1=ALU.add,
+                        out=normal, in0=token, scalar1=scale, scalar2=bias, op0=ALU.mult, op1=ALU.add
                     )
 
         def to_channels(i):
             u = i % 2
             if u == 0:
-                xn_turned[i // 2] = norm.tile([P, HALVES, 2, P, 2, 2], BF16, name="xn_turned", bufs=2)
+                xn_turned[i // 2] = norm.tile([P, HALVES, 2, P, 2, 2], BF16, name="xn_turned")
             for half in range(HALVES):
                 bank = banks.tile([P, PACK, P], F32, tag="bank", name="hat_bank")
                 for k in range(PACK):
@@ -316,16 +309,18 @@ def tile_swinmlpblocknew_pa_t_kernel(tc, x, norm1_w, norm1_b, spatial_w, spatial
         for step in range(-LOAD_LEAD, UNITS + OUT_LAG):
             for window in finished_windows(step - 2):
                 inverse_deviation(window)
-            if 0 <= step - OUT_LAG:
-                add_and_store(step - OUT_LAG)
             if last_window(step - QUANT_LAG):
                 quantise_tokens(step - QUANT_LAG)
+            if 0 <= step - OUT_LAG:
+                add_and_store(step - OUT_LAG)
             if 0 <= step - 1 < CHUNKS:
                 empty_weights(nc.vector.tensor_copy, step - 1, 1)
             if 0 <= step - 2 < CHUNKS:
                 quantise_weights(step - 2)
             for window in finished_windows(step - 1):
                 root(window)
+            if 0 <= step < TILES:
+                normalise(step, [PACK - 1])
             if 0 <= step - BACK_LAG < TILES:
                 to_tokens(step - BACK_LAG)
             if 0 <= step - TURN_LAG < TILES:
@@ -336,7 +331,7 @@ def tile_swinmlpblocknew_pa_t_kernel(tc, x, norm1_w, norm1_b, spatial_w, spatial
             if 0 <= step - MIX_LAG < UNITS:
                 multiply(step - MIX_LAG)
             if 0 <= step < TILES:
-                normalise(step)
+                normalise(step, range(PACK - 1))
             for window in finished_windows(step - 2):
                 normal_shift(window)
             for i in tiles_of_statistics(step):

from contextlib import ExitStack

import concourse.mybir as mybir
from concourse.masks import make_identity

F32 = mybir.dt.float32
BF16 = mybir.dt.bfloat16
U32 = mybir.dt.uint32
U8 = mybir.dt.uint8
FP8X4 = mybir.dt.float8_e4m3fn_x4
ALU = mybir.AluOpType
ACT = mybir.ActivationFunctionType

P = 128
PACK = 4
IMAGES = 4
WINDOWS = 4
TOKENS = 1024
PASSES = TOKENS // (P * PACK)
CHANNELS = 256
HALVES = CHANNELS // P
HEADS = 4
HEAD_DIM = CHANNELS // HEADS
EPS = 1e-5
COLS = WINDOWS * HEAD_DIM
RUN = TOKENS // P
GROUPS = 4
TILES_PER_IMAGE = 2 * WINDOWS
TILES = IMAGES * TILES_PER_IMAGE
UNITS = IMAGES * RUN
PAIRS = HEADS // 2
CHUNKS = RUN * PAIRS
STORE = 2
PSUM_BANKS = 8

STATS_LEAD = 3
TURN_LAG = 1
BACK_LAG = 4
QUANT_LAG = BACK_LAG + 1
MIX_LAG = TILES_PER_IMAGE - 1 + QUANT_LAG + 1
OUT_LAG = MIX_LAG + 1
LOAD_LEAD = 4

FLOPS = 2 * IMAGES * WINDOWS * HEADS * TOKENS * TOKENS * HEAD_DIM


def tile_swinmlpblocknew_pa_t_kernel(tc, x, norm1_w, norm1_b, spatial_w, spatial_b, out):
    nc = tc.nc

    x_cut = x.rearrange("b (wr r wc cg j) c -> b wc cg r wr (j c)", wr=2, r=32, wc=2, cg=GROUPS, j=RUN)
    out_cut = out.rearrange(
        "b (wr r wc cg k j) c -> b wc cg k r wr (j c)", wr=2, r=32, wc=2, cg=GROUPS, k=RUN // STORE, j=STORE
    )

    with ExitStack() as ctx:
        const = ctx.enter_context(tc.tile_pool(name="const", bufs=1))
        images = ctx.enter_context(tc.tile_pool(name="images", bufs=1))
        w_keep = ctx.enter_context(tc.tile_pool(name="w_keep", bufs=1))
        w_stage = ctx.enter_context(tc.tile_pool(name="w_stage", bufs=2))
        stats = ctx.enter_context(tc.tile_pool(name="stats", bufs=2 * WINDOWS))
        norm = ctx.enter_context(tc.tile_pool(name="norm", bufs=3))
        x_stage = ctx.enter_context(tc.tile_pool(name="x_stage", bufs=3))
        x_keep = ctx.enter_context(tc.tile_pool(name="x_keep", bufs=2 * PASSES))
        results = ctx.enter_context(tc.tile_pool(name="results", bufs=4))
        banks = ctx.enter_context(tc.psum_pool(name="banks", bufs=PSUM_BANKS))
        ctx.enter_context(tc.manual_schedule())

        def place(i):
            return i // TILES_PER_IMAGE, (i // 2) % WINDOWS, i % 2

        x_sb = [images.tile([P, WINDOWS * RUN * CHANNELS], BF16, name="x_sb%d" % b) for b in range(IMAGES)]

        def x_tokens(b):
            return x_sb[b][:].rearrange("p (n j c) -> p n j c", n=WINDOWS, j=RUN)

        def load_window(b, n):
            rows = x_sb[b][:].rearrange("p (n f) -> p n f", n=WINDOWS)
            for cg in range(GROUPS):
                nc.sync.dma_start(out=rows[cg:P:GROUPS, n, :], in_=x_cut[b, n // 2, cg][:, n % 2, :])

        bias_rows = const.tile([P, TOKENS], BF16, name="bias_rows")
        nc.scalar.dma_start(out=bias_rows[0:HEADS, :], in_=spatial_b)
        rows = const.tile([P, RUN, P], BF16, name="rows")
        nc.gpsimd.memset(rows[:], 0.0)
        gain_row, shift_row = HEADS, HEADS + HALVES
        nc.scalar.dma_start(
            out=rows[gain_row : gain_row + HALVES, 0, :], in_=norm1_w.rearrange("(a c) -> a c", a=HALVES)
        )
        nc.scalar.dma_start(
            out=rows[shift_row : shift_row + HALVES, 0, :], in_=norm1_b.rearrange("(a c) -> a c", a=HALVES)
        )
        ident_f32 = const.tile([P, P], F32, name="ident_f32")
        make_identity(nc, ident_f32[:])
        ident_bf16 = const.tile([P, P], BF16, name="ident_bf16")
        make_identity(nc, ident_bf16[:])
        nc.gpsimd.tensor_copy(
            out=rows[0:HEADS, :, :], in_=bias_rows[0:HEADS, :].rearrange("h (p j) -> h j p", j=RUN)
        )
        rows_turned = banks.tile([P, RUN, P], BF16, tag="bank", name="rows_turned")
        for plane in range(RUN):
            nc.tensor.transpose(rows_turned[:, plane, :], rows[:, plane, :], ident_bf16[:])
        columns = const.tile([P, RUN, HEADS + 2 * HALVES], F32, name="columns")
        nc.scalar.copy(out=columns[:], in_=rows_turned[:, :, 0 : HEADS + 2 * HALVES])

        def bias_column(h, j):
            return columns[:, j, h : h + 1]

        def gain_column(half):
            return columns[:, 0, gain_row + half : gain_row + half + 1]

        def shift_column(half):
            return columns[:, 0, shift_row + half : shift_row + half + 1]

        w_codes = w_keep.tile([P, CHUNKS, 2 * PASSES * P], U32, name="w_codes", align_bytes=64)
        w_scales = w_keep.tile([P, CHUNKS, 2 * PASSES * P], U8, name="w_scales", align_bytes=64)
        w_raw = {}
        w_grouped = {}
        w_banks = {}

        def load_weights(chunk):
            j, pair = chunk // PAIRS, chunk % PAIRS
            w_raw[chunk] = w_stage.tile([P, 2, TOKENS], BF16, name="w_raw", bufs=LOAD_LEAD)
            heads = spatial_w[2 * pair : 2 * pair + 2]
            nc.sync.dma_start(out=w_raw[chunk][:], in_=heads.rearrange("h (p j) t -> j p h t", j=RUN)[j])

        def turn_weights(chunk):
            w_grouped[chunk] = w_stage.tile([P, 2 * PASSES * P * PACK], BF16, name="w_grouped", bufs=3, align_bytes=64)
            words = w_raw[chunk][:].bitcast(F32).rearrange("p h (g q u) -> p h g q u", g=PASSES, u=2)
            for side in range(2):
                bank = banks.tile([P, PASSES, 2, P], F32, tag="bank", name="w_bank")
                for g in range(PASSES):
                    for u in range(2):
                        nc.tensor.transpose(bank[:, g, u, :], words[:, side, g, :, u], ident_f32[:])
                w_banks[chunk, side] = bank

        def empty_weights(engine_copy, chunk, side):
            grouped_words = w_grouped[chunk][:].bitcast(F32).rearrange("q (h g p u) -> q h g p u", h=2, g=PASSES, u=2)
            engine_copy(
                out=grouped_words[:, side], in_=w_banks[chunk, side][:].rearrange("q g u p -> q g p u")
            )

        def quantise_weights(chunk):
            nc.vector.quantize_mx(
                out=w_codes[:, chunk, :].bitcast(FP8X4), scales=w_scales[:, chunk, :], in_=w_grouped[chunk][:]
            )

        for n in range(WINDOWS):
            load_window(0, n)
            if n == 1:
                load_weights(0)

        moments = {}
        std = {}
        rstd = {}
        shift = {}

        def tile_statistics(i):
            b, n, u = place(i)
            window = i // 2
            if u == 0:
                moments[window] = stats.tile([P, RUN, 3], F32, name="moments")
            for j in (2 * u, 2 * u + 4):
                nc.vector.bn_stats(
                    out=moments[window][:, j : j + 2, :].rearrange("p t s -> p (t s)"),
                    in_=x_tokens(b)[:, n, j : j + 2, :].rearrange("p j c -> p c j"),
                )

        def root(window):
            std[window] = stats.tile([P, RUN, 1], F32, name="std")
            nc.scalar.activation(
                out=std[window][:],
                in_=moments[window][:, :, 2:3],
                func=ACT.Sqrt,
                scale=1.0 / CHANNELS,
                bias=EPS,
            )

        def inverse_deviation(window):
            rstd[window] = stats.tile([P, RUN, 1], F32, name="rstd")
            nc.vector.reciprocal(out=rstd[window][:], in_=std[window][:])

        def normal_shift(window):
            shift[window] = stats.tile([P, RUN, 1], F32, name="shift")
            nc.vector.scalar_tensor_tensor(
                out=shift[window][:],
                in0=moments[window][:, :, 1:2],
                scalar=-1.0,
                in1=rstd[window][:],
                op0=ALU.mult,
                op1=ALU.mult,
            )

        x_hat = {}
        xn_turned = {}
        x_grouped = {}
        x_codes = {}

        def normalise(i, places):
            b, n, u = place(i)
            window = i // 2
            if i not in x_hat:
                x_hat[i] = norm.tile([P, PACK, CHANNELS], F32, name="x_hat")
            for k in places:
                j = (2 * u, 2 * u + 1, 2 * u + 4, 2 * u + 5)[k]
                token, normal = x_tokens(b)[:, n, j, :], x_hat[i][:, k, :]
                scale, bias = rstd[window][:, j, :], shift[window][:, j, :]
                if k == PACK - 1:
                    nc.scalar.activation(out=normal, in_=token, func=ACT.Identity, scale=scale, bias=bias)
                else:
                    nc.gpsimd.tensor_scalar(
                        out=normal, in0=token, scalar1=scale, scalar2=bias, op0=ALU.mult, op1=ALU.add
                    )

        def to_channels(i):
            u = i % 2
            if u == 0:
                xn_turned[i // 2] = norm.tile([P, HALVES, 2, P, 2, 2], BF16, name="xn_turned")
            for half in range(HALVES):
                bank = banks.tile([P, PACK, P], F32, tag="bank", name="hat_bank")
                for k in range(PACK):
                    nc.tensor.transpose(bank[:, k, :], x_hat[i][:, k, half * P : (half + 1) * P], ident_f32[:])
                nc.scalar.activation(
                    out=xn_turned[i // 2][:, half, u],
                    in_=bank[:].rearrange("c (jh e) p -> c p jh e", jh=2),
                    func=ACT.Identity,
                    bias=shift_column(half),
                    scale=gain_column(half),
                )

        def to_tokens(i):
            b, n, g = place(i)
            words = xn_turned[i // 2][:].rearrange("c a u p jh e -> c (a u p jh e)").bitcast(F32)
            words = words.rearrange("c (a u g q) -> c a u g q", a=HALVES, u=2, g=PASSES)
            bank = banks.tile([P, 2, CHANNELS], F32, tag="bank", name="xn_bank")
            for u in range(2):
                for half in range(HALVES):
                    nc.tensor.transpose(bank[:, u, half * P : (half + 1) * P], words[:, half, u, g, :], ident_f32[:])
            if n == 0:
                x_grouped[b, g] = x_stage.tile([P, HEADS * COLS * PACK], BF16, name="x_grouped", align_bytes=64)
            grouped_words = (
                x_grouped[b, g][:].bitcast(F32).rearrange("q (h n d u) -> q h n d u", h=HEADS, n=WINDOWS, u=2)
            )
            nc.scalar.copy(out=grouped_words[:, :, n], in_=bank[:].rearrange("q u (h d) -> q h d u", h=HEADS))

        def quantise_tokens(i):
            b, n, g = place(i)
            codes = x_keep.tile([P, HEADS * COLS], U32, name="x_codes", align_bytes=64)
            scales = x_keep.tile([P, HEADS * COLS], U8, name="x_scales", align_bytes=64)
            nc.vector.quantize_mx(out=codes[:].bitcast(FP8X4), scales=scales[:], in_=x_grouped[b, g][:])
            x_codes[b, g] = (codes, scales)

        sums = {}
        result = {}

        def multiply(unit):
            b, j = unit // RUN, unit % RUN
            for pair in range(PAIRS):
                chunk = PAIRS * j + pair
                sums[unit, pair] = banks.tile([P, 2, COLS], F32, tag="bank", name="sum_bank")
                for side in range(2):
                    h = 2 * pair + side
                    for g in range(PASSES):
                        codes, scales = x_codes[b, g]
                        w_cols = slice((PASSES * side + g) * P, (PASSES * side + g + 1) * P)
                        x_cols = slice(h * COLS, (h + 1) * COLS)
                        nc.tensor.matmul_mx(
                            out=sums[unit, pair][:, side, :],
                            lhsT=w_codes[:, chunk, w_cols].bitcast(FP8X4),
                            lhsT_scale=w_scales[:, chunk, w_cols],
                            rhs=codes[:, x_cols].bitcast(FP8X4),
                            rhs_scale=scales[:, x_cols],
                            start=(g == 0),
                            stop=(g == PASSES - 1),
                        )

        def add_and_store(unit):
            b, j = unit // RUN, unit % RUN
            k = j % STORE
            if k == 0:
                result[unit // STORE] = results.tile([P, WINDOWS, STORE, CHANNELS], F32, name="result")
            res = result[unit // STORE]
            for h in range(HEADS):
                channels = slice(h * HEAD_DIM, (h + 1) * HEAD_DIM)
                nc.vector.scalar_tensor_tensor(
                    out=res[:, :, k, channels],
                    in0=sums[unit, h // 2][:, h % 2, :].rearrange("p (n d) -> p n d", n=WINDOWS),
                    scalar=bias_column(h, j),
                    in1=x_tokens(b)[:, :, j, channels],
                    op0=ALU.add,
                    op1=ALU.add,
                )
            if k == STORE - 1:
                runs = res[:].rearrange("p n k c -> p n (k c)")
                for wc in range(2):
                    for cg in range(GROUPS):
                        nc.sync.dma_start(
                            out=out_cut[b, wc, cg, j // STORE], in_=runs[cg:P:GROUPS, 2 * wc : 2 * wc + 2, :]
                        )

        def tiles_of_statistics(step):
            return [i for i in range(TILES) if 3 * i // 4 - STATS_LEAD == step]

        def finished_windows(step):
            return [i // 2 for i in tiles_of_statistics(step) if i % 2 == 1]

        def last_window(i):
            return 0 <= i < TILES and place(i)[1] == WINDOWS - 1

        for step in range(-LOAD_LEAD, UNITS + OUT_LAG):
            for window in finished_windows(step - 2):
                inverse_deviation(window)
            if last_window(step - QUANT_LAG):
                quantise_tokens(step - QUANT_LAG)
            if 0 <= step - OUT_LAG:
                add_and_store(step - OUT_LAG)
            if 0 <= step - 1 < CHUNKS:
                empty_weights(nc.vector.tensor_copy, step - 1, 1)
            if 0 <= step - 2 < CHUNKS:
                quantise_weights(step - 2)
            for window in finished_windows(step - 1):
                root(window)
            if 0 <= step < TILES:
                normalise(step, [PACK - 1])
            if 0 <= step - BACK_LAG < TILES:
                to_tokens(step - BACK_LAG)
            if 0 <= step - TURN_LAG < TILES:
                to_channels(step - TURN_LAG)
            if 0 <= step < CHUNKS:
                turn_weights(step)
                empty_weights(nc.scalar.copy, step, 0)
            if 0 <= step - MIX_LAG < UNITS:
                multiply(step - MIX_LAG)
            if 0 <= step < TILES:
                normalise(step, range(PACK - 1))
            for window in finished_windows(step - 2):
                normal_shift(window)
            for i in tiles_of_statistics(step):
                tile_statistics(i)
            chunk = step + LOAD_LEAD
            if 1 <= chunk < CHUNKS:
                load_weights(chunk)
            if 0 <= chunk < (IMAGES - 1) * WINDOWS:
                load_window(1 + chunk // WINDOWS, chunk % WINDOWS)
